import numpy as np
import ml_dtypes


def mxq(x, axis, fmt="e4m3"):
    dtype, down = {"e4m3": (ml_dtypes.float8_e4m3fn, 7), "e5m2": (ml_dtypes.float8_e5m2, 14)}[fmt]
    v = np.moveaxis(np.asarray(x, np.float32).astype(ml_dtypes.bfloat16).astype(np.float64), axis, -1)
    blocks = v.reshape(v.shape[:-1] + (-1, 32))
    amax = np.abs(blocks).max(-1, keepdims=True)
    byte = np.maximum(np.where(amax > 0, np.frexp(amax)[1] - 1 + 127, 0) - down, 1)
    scale = np.exp2(byte - 127.0)
    codes = (blocks / scale).astype(np.float32).astype(dtype).astype(np.float64)
    return np.moveaxis((codes * scale).reshape(v.shape), -1, axis)


WIDE = False


def mx_kscale(k):
    if not WIDE:
        return np.ones(k)
    levels = np.array([10, -10, 5, -5, 0])
    if k % 512:
        return np.exp2(np.random.permutation(np.resize(levels, k // 32))).repeat(32)
    a = np.empty((k // 512, 16))
    for p in range(k // 512):
        a[p, :8] = np.random.permutation(np.resize(levels, 8))
        for g in range(8):
            far = levels[np.abs(levels - a[p, g]) >= 10]
            a[p, g + 8] = far[np.random.randint(len(far))]
    return np.exp2(a.ravel()).repeat(32)


BF16 = ml_dtypes.bfloat16


def bf(x):
    return np.asarray(x, np.float32).astype(BF16)


def f64(x):
    return np.asarray(x).astype(np.float64)


B, T, KA, KT, DIM, NH, HD, E = 2, 512, 256, 256, 1024, 8, 128, 8
QC = 6.0


def setup_inputs():
    r = np.random.standard_normal
    s = mx_kscale(KA + KT)
    g = bf(1.0 + 0.25 * r(1))
    ratio = 1.0 / (1.0 + np.exp(-f64(g)[0]))
    sh = np.log(s) * np.sqrt(HD) / QC
    u = s.max() / s
    q_a, q_t = r((B, NH, T, HD)) * 1.2, r((B, NH, T, HD)) * 1.2
    k_a, k_t = r((B, NH, KA, HD)) * 1.2, r((B, NH, KT, HD)) * 1.2
    q_a[..., 0] = QC
    q_t[..., 0] = QC
    k_a[..., 0] += sh[:KA]
    k_t[..., 0] += sh[KA:] / ratio
    v_a = r((B, NH, KA, HD)) * 1.5 * u[:KA, None]
    v_t = r((B, NH, KT, HD)) * 1.5 * u[KA:, None]
    return {"q_a": bf(q_a), "q_t": bf(q_t), "k_a": bf(k_a), "k_t": bf(k_t),
            "v_a": bf(v_a), "v_t": bf(v_t), "gating_factor": g}


def reference(q_a, q_t, k_a, k_t, v_a, v_t, gating_factor):
    ratio_g = 1.0 / (1.0 + np.exp(-f64(gating_factor)))
    s_a = f64(q_a) @ f64(k_a).transpose(0, 1, 3, 2)
    s_t = (f64(q_t) @ f64(k_t).transpose(0, 1, 3, 2)) * ratio_g
    scores = np.concatenate([s_a, s_t], axis=-1) / np.sqrt(HD)
    e = np.exp(scores - scores.max(-1, keepdims=True))
    v = np.concatenate([f64(v_a), f64(v_t)], axis=2)
    out = (mxq(e, 3, "e4m3") @ mxq(v, 2, "e4m3")) / e.sum(-1, keepdims=True)
    return out.transpose(0, 2, 1, 3).reshape(B, T, NH * HD)

@@ -1,0 +1,274 @@
+import math
+from contextlib import ExitStack
+
+import concourse.mybir as mybir
+from concourse.masks import make_identity
+
+BF16 = mybir.dt.bfloat16
+F32 = mybir.dt.float32
+U32 = mybir.dt.uint32
+U8 = mybir.dt.uint8
+I32 = mybir.dt.int32
+FP8X4 = mybir.dt.float8_e4m3fn_x4
+ALU = mybir.AluOpType
+ACT = mybir.ActivationFunctionType
+AX = mybir.AxisListType
+
+P = 128
+HEADS = 16
+T = 512
+KS = 256
+D = 128
+NPAIR = 2 * HEADS
+C = 1.0 / math.sqrt(128.0)
+FLOPS = 4 * HEADS * T * (2 * KS) * D
+PIN = True
+T1S = 7
+NMV = 3
+EVV = 4
+CHUNKS = ((2, 4), (4, 8), (8, 12), (12, 16))
+
+
+def tile_l1regressionmoeactionhead_pb_kernel(tc, q_a, q_t, k_a, k_t, v_a, v_t, gating_factor, out):
+    nc = tc.nc
+    with ExitStack() as ctx:
+        if PIN:
+            ctx.enter_context(tc.manual_schedule())
+        res = ctx.enter_context(tc.tile_pool(name="res", bufs=1))
+        wk = ctx.enter_context(tc.tile_pool(name="wk", bufs=3))
+        ps_s = ctx.enter_context(tc.psum_pool(name="ps_s", bufs=3))
+        ps_tt = ctx.enter_context(tc.psum_pool(name="ps_tt", bufs=4))
+        ps_o = ctx.enter_context(tc.psum_pool(name="ps_o", bufs=1))
+
+        g_sb = res.tile([P, 1], BF16)
+        qa_sb = res.tile([P, HEADS * 512], BF16)
+        qt_sb = res.tile([P, HEADS * 512], BF16)
+        ka_sb = res.tile([P, HEADS * 256], BF16)
+        kt_sb = res.tile([P, HEADS * 256], BF16)
+        v_sb = res.tile([P, HEADS * 512], BF16)
+        vcodes = res.tile([P, HEADS * D], U32, align_bytes=64)
+        vscl = res.tile([P, HEADS * D], U8, align_bytes=64)
+        ident = res.tile([P, P], BF16)
+        eg = res.tile([P, 1], F32)
+        ratio = res.tile([P, 1], F32)
+        cr = res.tile([P, 1], F32)
+
+        nc.sync.dma_start(out=g_sb[:], in_=gating_factor.partition_broadcast(P))
+        qa_v = q_a.rearrange("b h (p j) d -> p (b h) (j d)", j=4)
+        qt_v = q_t.rearrange("b h (p j) d -> p (b h) (j d)", j=4)
+        ka_v = k_a.rearrange("b h (p j) d -> p (b h) (j d)", j=2)
+        kt_v = k_t.rearrange("b h (p j) d -> p (b h) (j d)", j=2)
+        va_v = v_a.rearrange("b h (p t) d -> p (b h) (t d)", t=4)
+        vt_v = v_t.rearrange("b h (p t) d -> p (b h) (t d)", t=4)
+        qa_s = qa_sb[:].rearrange("p (h x) -> p h x", x=512)
+        qt_s = qt_sb[:].rearrange("p (h x) -> p h x", x=512)
+        ka_s = ka_sb[:].rearrange("p (h x) -> p h x", x=256)
+        kt_s = kt_sb[:].rearrange("p (h x) -> p h x", x=256)
+        v_s = v_sb[:].rearrange("p (h x) -> p h x", x=512)
+        v_r = v_sb[:].rearrange("p (h t d) -> p h d t", t=4, d=D)
+        def load_kq(h0, h1):
+            nc.sync.dma_start(out=ka_s[:, h0:h1, :], in_=ka_v[:, h0:h1, :])
+            nc.sync.dma_start(out=qa_s[:, h0:h1, :], in_=qa_v[:, h0:h1, :])
+            nc.sync.dma_start(out=kt_s[:, h0:h1, :], in_=kt_v[:, h0:h1, :])
+            nc.sync.dma_start(out=qt_s[:, h0:h1, :], in_=qt_v[:, h0:h1, :])
+
+        def load_v(h0, h1):
+            nc.sync.dma_start(out=v_s[0:64, h0:h1, :], in_=va_v[:, h0:h1, :])
+            nc.sync.dma_start(out=v_s[64:128, h0:h1, :], in_=vt_v[:, h0:h1, :])
+
+        load_kq(0, 1)
+        load_kq(1, 2)
+        load_v(0, 2)
+        for h0, h1 in CHUNKS:
+            load_kq(h0, h1)
+            load_v(h0, h1)
+
+        make_identity(nc, ident[:])
+        nc.scalar.activation(out=eg[:], in_=g_sb[:], func=ACT.Exp, scale=-1.0)
+        nc.vector.tensor_scalar_add(out=eg[:], in0=eg[:], scalar1=1.0)
+        nc.vector.reciprocal(out=ratio[:], in_=eg[:])
+        nc.vector.tensor_scalar_mul(out=cr[:], in0=ratio[:], scalar1=C)
+
+        st = {}
+
+        def t1_pe(h, s):
+            q_sb, k_sb = (qa_sb, ka_sb) if s == 0 else (qt_sb, kt_sb)
+            t1 = ps_tt.tile([P, 1024], BF16, name="tt")
+            for j in range(4):
+                nc.tensor.transpose(t1[:, j * P:(j + 1) * P], q_sb[:, h * 512 + j * P:h * 512 + (j + 1) * P], ident[:])
+            for j in range(2):
+                nc.tensor.transpose(t1[:, 512 + j * P:512 + (j + 1) * P], k_sb[:, h * 256 + j * P:h * 256 + (j + 1) * P], ident[:])
+            st[("t1", h, s)] = t1
+
+        def t1_ev(h, s):
+            xT = wk.tile([P, 768], BF16, name="xT%d" % s, bufs=2)
+            if 1 <= 2 * h + s < T1S or (2 * h + s) % 4 == 0 and h > 0:
+                nc.scalar.copy(out=xT[:], in_=st[("t1", h, s)][:, 0:768])
+            else:
+                nc.vector.tensor_copy(out=xT[:], in_=st[("t1", h, s)][:, 0:768])
+            st[("xT", h, s)] = xT
+
+        def vprep(h):
+            if h % 4 == 0:
+                vg = wk.tile([P, 2048], BF16, name="vg", align_bytes=64, bufs=2)
+                st[("vg", h // 4)] = vg
+            vg = st[("vg", h // 4)]
+            lo = (h % 4) * 512
+            nc.gpsimd.tensor_scalar(out=vg[:, lo:lo + 512].rearrange("p (d t) -> p d t", t=4), in0=v_r[:, h],
+                                    scalar1=1.0, scalar2=0.0, op0=ALU.mult, op1=ALU.add)
+
+        def vquant(g):
+            nc.vector.quantize_mx(
+                out=vcodes[:, g * 512:(g + 1) * 512].bitcast(FP8X4),
+                scales=vscl[:, g * 512:(g + 1) * 512],
+                in_=st[("vg", g)][:],
+            )
+
+        def sc(s, jj):
+            h = s // 2
+            aT = st[("xT", h, 0)]
+            tT = st[("xT", h, 1)]
+            j = 2 * (s % 2) + jj
+            sb = ps_s.tile([P, 512], F32, name="sb")
+            nc.tensor.matmul(out=sb[:, 0:256], lhsT=aT[:, j * P:(j + 1) * P], rhs=aT[:, 512:768], start=True, stop=True)
+            nc.tensor.matmul(out=sb[:, 256:512], lhsT=tT[:, j * P:(j + 1) * P], rhs=tT[:, 512:768], start=True, stop=True)
+            st[("sb", s, jj)] = sb
+
+        def pre(s):
+            mxp = wk.tile([P, 4], F32, name="mxp", bufs=8)
+            nb = wk.tile([P, 2], F32, name="nb", bufs=8)
+            for jj in range(2):
+                sb = st[("sb", s, jj)]
+                x = wk.tile([P, 512], F32, name="x", bufs=10)
+                xv = x[:].rearrange("p (u e k) -> p u e k", u=2, e=2)
+                nc.vector.tensor_scalar(out=xv[:, :, :, 0:64], in0=sb[:, 0:256].rearrange("p (e k u) -> p u e k", e=2, u=2), scalar1=C, scalar2=None,
+                                        op0=ALU.mult, op1=ALU.max, accum_out=mxp[:, 2 * jj:2 * jj + 1])
+                nc.vector.tensor_scalar(out=xv[:, :, :, 64:128], in0=sb[:, 256:512].rearrange("p (e k u) -> p u e k", e=2, u=2), scalar1=cr[:, 0:1], scalar2=None,
+                                        op0=ALU.mult, op1=ALU.max, accum_out=mxp[:, 2 * jj + 1:2 * jj + 2])
+                st[("x", s, jj)] = x
+            nc.vector.tensor_reduce(out=nb[:], in_=mxp[:].rearrange("p (j u) -> p j u", u=2), axis=AX.X, op=ALU.max, negate=True)
+            st[("nb", s)] = nb
+
+        def ex(s):
+            h = s // 2
+            if s % 2 == 0:
+                rs = wk.tile([P, 4], F32, name="rs", bufs=8)
+                st[("rs", h)] = rs
+            rs = st[("rs", h)]
+            nb = st[("nb", s)]
+            e = wk.tile([P, 1024], BF16, name="e", bufs=5)
+            for jj in range(2):
+                j = 2 * (s % 2) + jj
+                nc.scalar.activation(out=e[:, jj * 512:(jj + 1) * 512], in_=st[("x", s, jj)][:], func=ACT.Exp,
+                                     bias=nb[:, jj:jj + 1], scale=1.0, accum_out=rs[:, j:j + 1])
+            st[("e", s)] = e
+
+        def te(s):
+            e = st[("e", s)]
+            t2 = ps_tt.tile([P, 1024], BF16, name="tt")
+            for i in range(8):
+                nc.tensor.transpose(t2[:, i * P:(i + 1) * P], e[:, i * P:(i + 1) * P], ident[:])
+            st[("t2", s)] = t2
+
+        def ev_v(s):
+            et = wk.tile([P, 512], BF16, name="et", bufs=4)
+            nc.vector.tensor_copy(out=et[:], in_=st[("t2", s)][:, 0:512])
+            st[("et", s)] = et
+
+        def ev_s(s):
+            t2 = st[("t2", s)]
+            if s % 2 == 0:
+                gr = wk.tile([P, 2048], BF16, name="gr", align_bytes=64, bufs=4)
+                st[("gr", s // 2)] = gr
+            gr = st[("gr", s // 2)]
+            b0 = (s % 2) * 1024
+            lo = 512 if (s % 2 == 0 or s >= NPAIR - EVV) else 0
+            if s >= NPAIR - EVV:
+                nc.vector.tensor_copy(out=gr[:, b0:b0 + 512].rearrange("p (q t) -> p q t", t=4),
+                                      in_=t2[:, 0:512].rearrange("p (t q) -> p q t", t=4))
+            nc.scalar.copy(out=gr[:, b0 + lo:b0 + 1024].rearrange("p (j q t) -> p j q t", q=P, t=4),
+                           in_=t2[:, lo:1024].rearrange("p (j t q) -> p j q t", q=P, t=4))
+
+        def rg(s):
+            b0 = (s % 2) * 1024
+            nc.gpsimd.tensor_scalar(
+                out=st[("gr", s // 2)][:, b0:b0 + 512].rearrange("p (q t) -> p q t", t=4),
+                in0=st[("et", s)][:].rearrange("p (t q) -> p q t", t=4),
+                scalar1=1.0, scalar2=0.0, op0=ALU.mult, op1=ALU.add,
+            )
+
+        def qz(h):
+            codes = wk.tile([P, 512], U32, name="codes", align_bytes=64, bufs=3)
+            scl = wk.tile([P, 512], U8, name="scl", align_bytes=64, bufs=3)
+            nc.vector.quantize_mx(out=codes[:].bitcast(FP8X4), scales=scl[:], in_=st[("gr", h)][:])
+            st[("cd", h)] = (codes, scl)
+
+        def mx(h):
+            o = ps_o.tile([P, 512], F32, name="o")
+            st[("o", h)] = o
+            codes, scl = st[("cd", h)]
+            for j in range(4):
+                nc.tensor.matmul_mx(
+                    out=o[:, j * D:(j + 1) * D],
+                    lhsT=codes[:, j * P:(j + 1) * P].bitcast(FP8X4),
+                    lhsT_scale=scl[:, j * P:(j + 1) * P],
+                    rhs=vcodes[:, h * D:(h + 1) * D].bitcast(FP8X4),
+                    rhs_scale=vscl[:, h * D:(h + 1) * D],
+                    start=True, stop=True,
+                )
+
+        def recip(h):
+            rinv = wk.tile([P, 4], F32, name="rinv", bufs=4)
+            nc.vector.reciprocal(out=rinv[:], in_=st[("rs", h)][:])
+            st[("rinv", h)] = rinv
+
+        def nm(h):
+            rinv = st[("rinv", h)]
+            o = st[("o", h)]
+            osb = wk.tile([P, 512], F32, name="osb")
+            if h >= HEADS - NMV:
+                nc.vector.tensor_tensor(out=osb[:].rearrange("p (j d) -> p j d", d=D), in0=o[:].rearrange("p (j d) -> p j d", d=D),
+                                        in1=rinv[:].unsqueeze(2).to_broadcast([P, 4, D]), op=ALU.mult)
+            for j in range(4 if h < HEADS - NMV else 0):
+                nc.scalar.activation(out=osb[:, j * D:(j + 1) * D], in_=o[:, j * D:(j + 1) * D], func=ACT.Copy, scale=rinv[:, j:j + 1])
+            n, hh = divmod(h, 8)
+            nc.sync.dma_start(
+                out=out[n].rearrange("(p j) c -> p j c", j=4)[:, :, hh * D:(hh + 1) * D],
+                in_=osb[:].rearrange("p (j d) -> p j d", d=D),
+            )
+
+        for t in range(-6, NPAIR + 7):
+            if t % 2 == 1 and 0 <= (t - 5) // 2 < HEADS:
+                recip((t - 5) // 2)
+            if t % 2 == 0 and 0 <= (t - 6) // 2 < HEADS:
+                qz((t - 6) // 2)
+            if (t - 6) % 4 == 0 and 0 <= (t - 6) // 4 < HEADS // 4:
+                vquant((t - 6) // 4)
+            if 0 <= t + 2 < NPAIR:
+                sc(t + 2, 1)
+            if t < 0 and 0 <= t + 3 < NPAIR:
+                sc(t + 3, 0)
+            if 0 <= t - 1 < NPAIR:
+                te(t - 1)
+            if 0 <= t + 6 < 2 * HEADS:
+                t1_pe((t + 6) // 2, (t + 6) % 2)
+            if t >= 0 and 0 <= t + 3 < NPAIR:
+                sc(t + 3, 0)
+            if t % 2 == 1 and 0 <= (t - 7) // 2 < HEADS:
+                mx((t - 7) // 2)
+            if 0 <= t + 5 < 2 * HEADS:
+                t1_ev((t + 5) // 2, (t + 5) % 2)
+            if 0 <= t - 2 < NPAIR - EVV and (t - 2) % 2 == 0:
+                ev_v(t - 2)
+            if 0 <= t + 2 < NPAIR:
+                pre(t + 2)
+            if 0 <= t < NPAIR:
+                ex(t)
+            if 0 <= t - 2 < NPAIR:
+                ev_s(t - 2)
+            if t % 2 == 0 and 0 <= (t - 8) // 2 < HEADS:
+                nm((t - 8) // 2)
+            if 0 <= t - 3 < NPAIR - EVV and (t - 3) % 2 == 0:
+                rg(t - 3)
+            if 0 <= t - 1 < HEADS:
+                vprep(t - 1)

@@ -8,11 +8,9 @@ BF16 = mybir.dt.bfloat16
 F32 = mybir.dt.float32
 U32 = mybir.dt.uint32
 U8 = mybir.dt.uint8
-I32 = mybir.dt.int32
 FP8X4 = mybir.dt.float8_e4m3fn_x4
 ALU = mybir.AluOpType
 ACT = mybir.ActivationFunctionType
-AX = mybir.AxisListType
 
 P = 128
 HEADS = 16
@@ -20,24 +18,20 @@ T = 512
 KS = 256
 D = 128
 NPAIR = 2 * HEADS
+NSET = 2 * HEADS
 C = 1.0 / math.sqrt(128.0)
 FLOPS = 4 * HEADS * T * (2 * KS) * D
-PIN = True
-T1S = 7
-NMV = 3
-EVV = 4
 CHUNKS = ((2, 4), (4, 8), (8, 12), (12, 16))
 
 
 def tile_l1regressionmoeactionhead_pb_kernel(tc, q_a, q_t, k_a, k_t, v_a, v_t, gating_factor, out):
     nc = tc.nc
     with ExitStack() as ctx:
-        if PIN:
-            ctx.enter_context(tc.manual_schedule())
+        ctx.enter_context(tc.manual_schedule())
         res = ctx.enter_context(tc.tile_pool(name="res", bufs=1))
         wk = ctx.enter_context(tc.tile_pool(name="wk", bufs=3))
-        ps_s = ctx.enter_context(tc.psum_pool(name="ps_s", bufs=3))
-        ps_tt = ctx.enter_context(tc.psum_pool(name="ps_tt", bufs=4))
+        ps_s = ctx.enter_context(tc.psum_pool(name="ps_s", bufs=4))
+        ps_t = ctx.enter_context(tc.psum_pool(name="ps_t", bufs=3))
         ps_o = ctx.enter_context(tc.psum_pool(name="ps_o", bufs=1))
 
         g_sb = res.tile([P, 1], BF16)
@@ -49,11 +43,12 @@ def tile_l1regressionmoeactionhead_pb_kernel(tc, q_a, q_t, k_a, k_t, v_a, v_t, g
         vcodes = res.tile([P, HEADS * D], U32, align_bytes=64)
         vscl = res.tile([P, HEADS * D], U8, align_bytes=64)
         ident = res.tile([P, P], BF16)
+        ident32 = res.tile([P, P], F32)
         eg = res.tile([P, 1], F32)
+        eg1 = res.tile([P, 1], F32)
         ratio = res.tile([P, 1], F32)
-        cr = res.tile([P, 1], F32)
+        ncr = res.tile([P, 1], F32)
 
-        nc.sync.dma_start(out=g_sb[:], in_=gating_factor.partition_broadcast(P))
         qa_v = q_a.rearrange("b h (p j) d -> p (b h) (j d)", j=4)
         qt_v = q_t.rearrange("b h (p j) d -> p (b h) (j d)", j=4)
         ka_v = k_a.rearrange("b h (p j) d -> p (b h) (j d)", j=2)
@@ -66,6 +61,7 @@ def tile_l1regressionmoeactionhead_pb_kernel(tc, q_a, q_t, k_a, k_t, v_a, v_t, g
         kt_s = kt_sb[:].rearrange("p (h x) -> p h x", x=256)
         v_s = v_sb[:].rearrange("p (h x) -> p h x", x=512)
         v_r = v_sb[:].rearrange("p (h t d) -> p h d t", t=4, d=D)
+
         def load_kq(h0, h1):
             nc.sync.dma_start(out=ka_s[:, h0:h1, :], in_=ka_v[:, h0:h1, :])
             nc.sync.dma_start(out=qa_s[:, h0:h1, :], in_=qa_v[:, h0:h1, :])
@@ -76,6 +72,7 @@ def tile_l1regressionmoeactionhead_pb_kernel(tc, q_a, q_t, k_a, k_t, v_a, v_t, g
             nc.sync.dma_start(out=v_s[0:64, h0:h1, :], in_=va_v[:, h0:h1, :])
             nc.sync.dma_start(out=v_s[64:128, h0:h1, :], in_=vt_v[:, h0:h1, :])
 
+        nc.scalar.dma_start(out=g_sb[:], in_=gating_factor.partition_broadcast(P))
         load_kq(0, 1)
         load_kq(1, 2)
         load_v(0, 2)
@@ -84,37 +81,38 @@ def tile_l1regressionmoeactionhead_pb_kernel(tc, q_a, q_t, k_a, k_t, v_a, v_t, g
             load_v(h0, h1)
 
         make_identity(nc, ident[:])
+        make_identity(nc, ident32[:])
         nc.scalar.activation(out=eg[:], in_=g_sb[:], func=ACT.Exp, scale=-1.0)
-        nc.vector.tensor_scalar_add(out=eg[:], in0=eg[:], scalar1=1.0)
-        nc.vector.reciprocal(out=ratio[:], in_=eg[:])
-        nc.vector.tensor_scalar_mul(out=cr[:], in0=ratio[:], scalar1=C)
+        nc.vector.tensor_scalar_add(out=eg1[:], in0=eg[:], scalar1=1.0)
+        nc.vector.reciprocal(out=ratio[:], in_=eg1[:])
+        nc.vector.tensor_scalar_mul(out=ncr[:], in0=ratio[:], scalar1=-C)
 
         st = {}
 
-        def t1_pe(h, s):
+        def t1_pe(n):
+            h, s = divmod(n, 2)
             q_sb, k_sb = (qa_sb, ka_sb) if s == 0 else (qt_sb, kt_sb)
-            t1 = ps_tt.tile([P, 1024], BF16, name="tt")
-            for j in range(4):
-                nc.tensor.transpose(t1[:, j * P:(j + 1) * P], q_sb[:, h * 512 + j * P:h * 512 + (j + 1) * P], ident[:])
+            t1 = ps_t.tile([P, 1024], BF16, name="tt")
             for j in range(2):
                 nc.tensor.transpose(t1[:, 512 + j * P:512 + (j + 1) * P], k_sb[:, h * 256 + j * P:h * 256 + (j + 1) * P], ident[:])
-            st[("t1", h, s)] = t1
+            for j in range(4):
+                nc.tensor.transpose(t1[:, j * P:(j + 1) * P], q_sb[:, h * 512 + j * P:h * 512 + (j + 1) * P], ident[:])
+            st[("t1", n)] = t1
 
-        def t1_ev(h, s):
-            xT = wk.tile([P, 768], BF16, name="xT%d" % s, bufs=2)
-            if 1 <= 2 * h + s < T1S or (2 * h + s) % 4 == 0 and h > 0:
-                nc.scalar.copy(out=xT[:], in_=st[("t1", h, s)][:, 0:768])
+        def t1_ev(n):
+            xT = wk.tile([P, 768], BF16, name="xT%d" % (n % 2), bufs=3)
+            if n < 4 and n % 2 == 0:
+                nc.vector.tensor_copy(out=xT[:], in_=st[("t1", n)][:, 0:768])
             else:
-                nc.vector.tensor_copy(out=xT[:], in_=st[("t1", h, s)][:, 0:768])
-            st[("xT", h, s)] = xT
+                nc.scalar.copy(out=xT[:], in_=st[("t1", n)][:, 0:768])
+            st[("xT", n)] = xT
 
         def vprep(h):
             if h % 4 == 0:
-                vg = wk.tile([P, 2048], BF16, name="vg", align_bytes=64, bufs=2)
+                vg = wk.tile([P, 2048], BF16, name="vg", align_bytes=64, bufs=4)
                 st[("vg", h // 4)] = vg
-            vg = st[("vg", h // 4)]
             lo = (h % 4) * 512
-            nc.gpsimd.tensor_scalar(out=vg[:, lo:lo + 512].rearrange("p (d t) -> p d t", t=4), in0=v_r[:, h],
+            nc.gpsimd.tensor_scalar(out=st[("vg", h // 4)][:, lo:lo + 512].rearrange("p (d t) -> p d t", t=4), in0=v_r[:, h],
                                     scalar1=1.0, scalar2=0.0, op0=ALU.mult, op1=ALU.add)
 
         def vquant(g):
@@ -126,8 +124,8 @@ def tile_l1regressionmoeactionhead_pb_kernel(tc, q_a, q_t, k_a, k_t, v_a, v_t, g
 
         def sc(s, jj):
             h = s // 2
-            aT = st[("xT", h, 0)]
-            tT = st[("xT", h, 1)]
+            aT = st[("xT", 2 * h)]
+            tT = st[("xT", 2 * h + 1)]
             j = 2 * (s % 2) + jj
             sb = ps_s.tile([P, 512], F32, name="sb")
             nc.tensor.matmul(out=sb[:, 0:256], lhsT=aT[:, j * P:(j + 1) * P], rhs=aT[:, 512:768], start=True, stop=True)
@@ -135,67 +133,49 @@ def tile_l1regressionmoeactionhead_pb_kernel(tc, q_a, q_t, k_a, k_t, v_a, v_t, g
             st[("sb", s, jj)] = sb
 
         def pre(s):
-            mxp = wk.tile([P, 4], F32, name="mxp", bufs=8)
-            nb = wk.tile([P, 2], F32, name="nb", bufs=8)
+            na = wk.tile([P, 2], F32, name="na", bufs=4)
+            nb = wk.tile([P, 2], F32, name="nb", bufs=4)
+            xs = []
             for jj in range(2):
-                sb = st[("sb", s, jj)]
-                x = wk.tile([P, 512], F32, name="x", bufs=10)
-                xv = x[:].rearrange("p (u e k) -> p u e k", u=2, e=2)
-                nc.vector.tensor_scalar(out=xv[:, :, :, 0:64], in0=sb[:, 0:256].rearrange("p (e k u) -> p u e k", e=2, u=2), scalar1=C, scalar2=None,
-                                        op0=ALU.mult, op1=ALU.max, accum_out=mxp[:, 2 * jj:2 * jj + 1])
-                nc.vector.tensor_scalar(out=xv[:, :, :, 64:128], in0=sb[:, 256:512].rearrange("p (e k u) -> p u e k", e=2, u=2), scalar1=cr[:, 0:1], scalar2=None,
-                                        op0=ALU.mult, op1=ALU.max, accum_out=mxp[:, 2 * jj + 1:2 * jj + 2])
+                x = wk.tile([P, 512], F32, name="x", bufs=6)
+                xs.append(x)
                 st[("x", s, jj)] = x
-            nc.vector.tensor_reduce(out=nb[:], in_=mxp[:].rearrange("p (j u) -> p j u", u=2), axis=AX.X, op=ALU.max, negate=True)
+                nc.vector.tensor_scalar(out=x[:].rearrange("p (u k e) -> p u k e", u=2, e=2)[:, :, 0:64, :],
+                                        in0=st[("sb", s, jj)][:, 0:256].rearrange("p (e k u) -> p u k e", e=2, u=2),
+                                        scalar1=-C, scalar2=None, op0=ALU.mult, op1=ALU.min, accum_out=na[:, jj:jj + 1])
+            for jj in range(2):
+                nc.vector.tensor_scalar(out=xs[jj][:].rearrange("p (u k e) -> p u k e", u=2, e=2)[:, :, 64:128, :],
+                                        in0=st[("sb", s, jj)][:, 256:512].rearrange("p (e k u) -> p u k e", e=2, u=2),
+                                        scalar1=ncr[:, 0:1], scalar2=na[:, jj:jj + 1], op0=ALU.mult, op1=ALU.min, accum_out=nb[:, jj:jj + 1])
             st[("nb", s)] = nb
 
         def ex(s):
             h = s // 2
             if s % 2 == 0:
-                rs = wk.tile([P, 4], F32, name="rs", bufs=8)
+                rs = wk.tile([P, 4], F32, name="rs", bufs=4)
                 st[("rs", h)] = rs
-            rs = st[("rs", h)]
             nb = st[("nb", s)]
-            e = wk.tile([P, 1024], BF16, name="e", bufs=5)
+            e = wk.tile([P, 1024], BF16, name="e", bufs=3)
             for jj in range(2):
                 j = 2 * (s % 2) + jj
                 nc.scalar.activation(out=e[:, jj * 512:(jj + 1) * 512], in_=st[("x", s, jj)][:], func=ACT.Exp,
-                                     bias=nb[:, jj:jj + 1], scale=1.0, accum_out=rs[:, j:j + 1])
+                                     bias=nb[:, jj:jj + 1], scale=-1.0, accum_out=st[("rs", h)][:, j:j + 1])
             st[("e", s)] = e
 
         def te(s):
-            e = st[("e", s)]
-            t2 = ps_tt.tile([P, 1024], BF16, name="tt")
-            for i in range(8):
-                nc.tensor.transpose(t2[:, i * P:(i + 1) * P], e[:, i * P:(i + 1) * P], ident[:])
+            words = st[("e", s)][:].bitcast(F32)
+            t2 = ps_t.tile([P, 512], F32, name="tt")
+            for i in range(4):
+                nc.tensor.transpose(t2[:, i * P:(i + 1) * P], words[:, i * P:(i + 1) * P], ident32[:])
             st[("t2", s)] = t2
 
-        def ev_v(s):
-            et = wk.tile([P, 512], BF16, name="et", bufs=4)
-            nc.vector.tensor_copy(out=et[:], in_=st[("t2", s)][:, 0:512])
-            st[("et", s)] = et
-
-        def ev_s(s):
-            t2 = st[("t2", s)]
+        def ev(s):
             if s % 2 == 0:
-                gr = wk.tile([P, 2048], BF16, name="gr", align_bytes=64, bufs=4)
+                gr = wk.tile([P, 2048], BF16, name="gr", align_bytes=64, bufs=3)
                 st[("gr", s // 2)] = gr
-            gr = st[("gr", s // 2)]
-            b0 = (s % 2) * 1024
-            lo = 512 if (s % 2 == 0 or s >= NPAIR - EVV) else 0
-            if s >= NPAIR - EVV:
-                nc.vector.tensor_copy(out=gr[:, b0:b0 + 512].rearrange("p (q t) -> p q t", t=4),
-                                      in_=t2[:, 0:512].rearrange("p (t q) -> p q t", t=4))
-            nc.scalar.copy(out=gr[:, b0 + lo:b0 + 1024].rearrange("p (j q t) -> p j q t", q=P, t=4),
-                           in_=t2[:, lo:1024].rearrange("p (j t q) -> p j q t", q=P, t=4))
-
-        def rg(s):
-            b0 = (s % 2) * 1024
-            nc.gpsimd.tensor_scalar(
-                out=st[("gr", s // 2)][:, b0:b0 + 512].rearrange("p (q t) -> p q t", t=4),
-                in0=st[("et", s)][:].rearrange("p (t q) -> p q t", t=4),
-                scalar1=1.0, scalar2=0.0, op0=ALU.mult, op1=ALU.add,
-            )
+            b0 = (s % 2) * 512
+            nc.scalar.copy(out=st[("gr", s // 2)][:].bitcast(F32)[:, b0:b0 + 512].rearrange("p (j q u) -> p j q u", j=2, u=2),
+                           in_=st[("t2", s)][:].rearrange("p (j u q) -> p j q u", j=2, u=2))
 
         def qz(h):
             codes = wk.tile([P, 512], U32, name="codes", align_bytes=64, bufs=3)
@@ -223,52 +203,41 @@ def tile_l1regressionmoeactionhead_pb_kernel(tc, q_a, q_t, k_a, k_t, v_a, v_t, g
             st[("rinv", h)] = rinv
 
         def nm(h):
-            rinv = st[("rinv", h)]
-            o = st[("o", h)]
-            osb = wk.tile([P, 512], F32, name="osb")
-            if h >= HEADS - NMV:
-                nc.vector.tensor_tensor(out=osb[:].rearrange("p (j d) -> p j d", d=D), in0=o[:].rearrange("p (j d) -> p j d", d=D),
-                                        in1=rinv[:].unsqueeze(2).to_broadcast([P, 4, D]), op=ALU.mult)
-            for j in range(4 if h < HEADS - NMV else 0):
-                nc.scalar.activation(out=osb[:, j * D:(j + 1) * D], in_=o[:, j * D:(j + 1) * D], func=ACT.Copy, scale=rinv[:, j:j + 1])
+            osb = wk.tile([P, 512], F32, name="osb", bufs=4)
+            nc.vector.tensor_tensor(out=osb[:].rearrange("p (j d) -> p j d", d=D), in0=st[("o", h)][:].rearrange("p (j d) -> p j d", d=D),
+                                    in1=st[("rinv", h)][:].unsqueeze(2).to_broadcast([P, 4, D]), op=ALU.mult)
             n, hh = divmod(h, 8)
             nc.sync.dma_start(
                 out=out[n].rearrange("(p j) c -> p j c", j=4)[:, :, hh * D:(hh + 1) * D],
                 in_=osb[:].rearrange("p (j d) -> p j d", d=D),
             )
 
-        for t in range(-6, NPAIR + 7):
-            if t % 2 == 1 and 0 <= (t - 5) // 2 < HEADS:
-                recip((t - 5) // 2)
-            if t % 2 == 0 and 0 <= (t - 6) // 2 < HEADS:
-                qz((t - 6) // 2)
-            if (t - 6) % 4 == 0 and 0 <= (t - 6) // 4 < HEADS // 4:
-                vquant((t - 6) // 4)
-            if 0 <= t + 2 < NPAIR:
-                sc(t + 2, 1)
-            if t < 0 and 0 <= t + 3 < NPAIR:
-                sc(t + 3, 0)
+        for t in range(-5, NPAIR + 5):
             if 0 <= t - 1 < NPAIR:
                 te(t - 1)
-            if 0 <= t + 6 < 2 * HEADS:
-                t1_pe((t + 6) // 2, (t + 6) % 2)
-            if t >= 0 and 0 <= t + 3 < NPAIR:
-                sc(t + 3, 0)
-            if t % 2 == 1 and 0 <= (t - 7) // 2 < HEADS:
-                mx((t - 7) // 2)
-            if 0 <= t + 5 < 2 * HEADS:
-                t1_ev((t + 5) // 2, (t + 5) % 2)
-            if 0 <= t - 2 < NPAIR - EVV and (t - 2) % 2 == 0:
-                ev_v(t - 2)
+            if t % 2 == 0 and 0 <= (t - 4) // 2 < HEADS:
+                mx((t - 4) // 2)
             if 0 <= t + 2 < NPAIR:
-                pre(t + 2)
+                sc(t + 2, 0)
+                sc(t + 2, 1)
+            if 0 <= t + 5 < NSET:
+                t1_pe(t + 5)
+            if 0 <= t + 1 < NPAIR:
+                pre(t + 1)
+            if t % 2 == 1 and 0 <= (t - 3) // 2 < HEADS:
+                qz((t - 3) // 2)
+                recip((t - 3) // 2)
+            if (t - 2) % 8 == 0 and 0 <= (t - 2) // 8 < HEADS // 4:
+                vquant((t - 2) // 8)
+            if t % 2 == 0 and 0 <= (t - 4) // 2 < HEADS:
+                nm((t - 4) // 2)
+            if t < 0 and 0 <= t + 5 < NSET:
+                t1_ev(t + 5)
             if 0 <= t < NPAIR:
                 ex(t)
-            if 0 <= t - 2 < NPAIR:
-                ev_s(t - 2)
-            if t % 2 == 0 and 0 <= (t - 8) // 2 < HEADS:
-                nm((t - 8) // 2)
-            if 0 <= t - 3 < NPAIR - EVV and (t - 3) % 2 == 0:
-                rg(t - 3)
-            if 0 <= t - 1 < HEADS:
-                vprep(t - 1)
+            if 0 <= t - 1 < NPAIR:
+                ev(t - 1)
+            if t >= 0 and 0 <= t + 5 < NSET:
+                t1_ev(t + 5)
+            if 0 <= t + 3 < HEADS:
+                vprep(t + 3)

@@ -31,8 +31,7 @@ def tile_l1regressionmoeactionhead_pb_kernel(tc, q_a, q_t, k_a, k_t, v_a, v_t, g
         res = ctx.enter_context(tc.tile_pool(name="res", bufs=1))
         wk = ctx.enter_context(tc.tile_pool(name="wk", bufs=3))
         ps_s = ctx.enter_context(tc.psum_pool(name="ps_s", bufs=4))
-        ps_t = ctx.enter_context(tc.psum_pool(name="ps_t", bufs=3))
-        ps_o = ctx.enter_context(tc.psum_pool(name="ps_o", bufs=1))
+        ps_t = ctx.enter_context(tc.psum_pool(name="ps_t", bufs=4))
 
         g_sb = res.tile([P, 1], BF16)
         qa_sb = res.tile([P, HEADS * 512], BF16)
@@ -184,7 +183,7 @@ def tile_l1regressionmoeactionhead_pb_kernel(tc, q_a, q_t, k_a, k_t, v_a, v_t, g
             st[("cd", h)] = (codes, scl)
 
         def mx(h):
-            o = ps_o.tile([P, 512], F32, name="o")
+            o = ps_t.tile([P, 512], F32, name="tt")
             st[("o", h)] = o
             codes, scl = st[("cd", h)]
             for j in range(4):
@@ -212,7 +211,7 @@ def tile_l1regressionmoeactionhead_pb_kernel(tc, q_a, q_t, k_a, k_t, v_a, v_t, g
                 in_=osb[:].rearrange("p (j d) -> p j d", d=D),
             )
 
-        for t in range(-5, NPAIR + 5):
+        for t in range(-6, NPAIR + 5):
             if 0 <= t - 1 < NPAIR:
                 te(t - 1)
             if t % 2 == 0 and 0 <= (t - 4) // 2 < HEADS:
@@ -220,8 +219,8 @@ def tile_l1regressionmoeactionhead_pb_kernel(tc, q_a, q_t, k_a, k_t, v_a, v_t, g
             if 0 <= t + 2 < NPAIR:
                 sc(t + 2, 0)
                 sc(t + 2, 1)
-            if 0 <= t + 5 < NSET:
-                t1_pe(t + 5)
+            if 0 <= t + 6 < NSET:
+                t1_pe(t + 6)
             if 0 <= t + 1 < NPAIR:
                 pre(t + 1)
             if t % 2 == 1 and 0 <= (t - 3) // 2 < HEADS:

@@ -21,6 +21,8 @@ NPAIR = 2 * HEADS
 NSET = 2 * HEADS
 C = 1.0 / math.sqrt(128.0)
 FLOPS = 4 * HEADS * T * (2 * KS) * D
+NWARM = 3
+NM_S = (1, 4, 7, 10)
 CHUNKS = ((2, 4), (4, 8), (8, 12), (12, 16))
 
 
@@ -42,8 +44,10 @@ def tile_l1regressionmoeactionhead_pb_kernel(tc, q_a, q_t, k_a, k_t, v_a, v_t, g
         vcodes = res.tile([P, HEADS * D], U32, align_bytes=64)
         vscl = res.tile([P, HEADS * D], U8, align_bytes=64)
         ident = res.tile([P, P], BF16)
+        zeros = res.tile([P, 512], BF16)
         ident32 = res.tile([P, P], F32)
         eg = res.tile([P, 1], F32)
+        dummy = res.tile([P, 1], F32)
         eg1 = res.tile([P, 1], F32)
         ratio = res.tile([P, 1], F32)
         ncr = res.tile([P, 1], F32)
@@ -81,30 +85,37 @@ def tile_l1regressionmoeactionhead_pb_kernel(tc, q_a, q_t, k_a, k_t, v_a, v_t, g
 
         make_identity(nc, ident[:])
         make_identity(nc, ident32[:])
-        nc.scalar.activation(out=eg[:], in_=g_sb[:], func=ACT.Exp, scale=-1.0)
-        nc.vector.tensor_scalar_add(out=eg1[:], in0=eg[:], scalar1=1.0)
-        nc.vector.reciprocal(out=ratio[:], in_=eg1[:])
-        nc.vector.tensor_scalar_mul(out=ncr[:], in0=ratio[:], scalar1=-C)
+        nc.vector.memset(zeros[:], 0.0)
+        nc.vector.memset(eg[:], 0.0)
+        nc.scalar.activation(out=dummy[:], in_=eg[:], func=ACT.Exp)
 
         st = {}
 
-        def t1_pe(n):
+        def t1_pe(n, lo=0, hi=6):
             h, s = divmod(n, 2)
             q_sb, k_sb = (qa_sb, ka_sb) if s == 0 else (qt_sb, kt_sb)
             t1 = ps_t.tile([P, 1024], BF16, name="tt")
-            for j in range(2):
-                nc.tensor.transpose(t1[:, 512 + j * P:512 + (j + 1) * P], k_sb[:, h * 256 + j * P:h * 256 + (j + 1) * P], ident[:])
-            for j in range(4):
-                nc.tensor.transpose(t1[:, j * P:(j + 1) * P], q_sb[:, h * 512 + j * P:h * 512 + (j + 1) * P], ident[:])
-            st[("t1", n)] = t1
+            for i in range(lo, hi):
+                src = k_sb[:, h * 256 + i * P:h * 256 + (i + 1) * P] if i < 2 else q_sb[:, h * 512 + (i - 2) * P:h * 512 + (i - 1) * P]
+                nc.tensor.transpose(t1[:, i * P:(i + 1) * P], src, ident[:])
+            st[("t1", n, lo)] = t1
 
-        def t1_ev(n):
-            xT = wk.tile([P, 768], BF16, name="xT%d" % (n % 2), bufs=3)
-            if n < 4 and n % 2 == 0:
-                nc.vector.tensor_copy(out=xT[:], in_=st[("t1", n)][:, 0:768])
+        def t1_ev(n, lo=0, hi=6, vec=False):
+            if lo == 0:
+                xT = wk.tile([P, 768], BF16, name="xT%d" % (n % 2), bufs=3)
+                st[("xT", n)] = xT
+            dst = st[("xT", n)][:, lo * P:hi * P]
+            src = st[("t1", n, lo)][:, lo * P:hi * P]
+            if vec:
+                nc.vector.tensor_copy(out=dst, in_=src)
             else:
-                nc.scalar.copy(out=xT[:], in_=st[("t1", n)][:, 0:768])
-            st[("xT", n)] = xT
+                nc.scalar.copy(out=dst, in_=src)
+
+        def gate():
+            nc.scalar.activation(out=eg[:], in_=g_sb[:], func=ACT.Exp, scale=-1.0)
+            nc.vector.tensor_scalar_add(out=eg1[:], in0=eg[:], scalar1=1.0)
+            nc.vector.reciprocal(out=ratio[:], in_=eg1[:])
+            nc.vector.tensor_scalar_mul(out=ncr[:], in0=ratio[:], scalar1=-C)
 
         def vprep(h):
             if h % 4 == 0:
@@ -121,29 +132,36 @@ def tile_l1regressionmoeactionhead_pb_kernel(tc, q_a, q_t, k_a, k_t, v_a, v_t, g
                 in_=st[("vg", g)][:],
             )
 
-        def sc(s, jj):
-            h = s // 2
-            aT = st[("xT", 2 * h)]
-            tT = st[("xT", 2 * h + 1)]
-            j = 2 * (s % 2) + jj
+        def bank(s, jj):
             sb = ps_s.tile([P, 512], F32, name="sb")
-            nc.tensor.matmul(out=sb[:, 0:256], lhsT=aT[:, j * P:(j + 1) * P], rhs=aT[:, 512:768], start=True, stop=True)
-            nc.tensor.matmul(out=sb[:, 256:512], lhsT=tT[:, j * P:(j + 1) * P], rhs=tT[:, 512:768], start=True, stop=True)
             st[("sb", s, jj)] = sb
 
-        def pre(s):
+        def keep_warm(t2):
+            nc.tensor.matmul_mx(out=t2[:], lhsT=vcodes[:, 0:P].bitcast(FP8X4), lhsT_scale=vscl[:, 0:P],
+                                rhs=vcodes[:, 0:512].bitcast(FP8X4), rhs_scale=vscl[:, 0:512], start=True, stop=True)
+
+        def sc(s, jj, halves=(0, 1)):
+            h = s // 2
+            j = 2 * (s % 2) + jj
+            for half in halves:
+                xT = st[("xT", 2 * h + half)]
+                nc.tensor.matmul(out=st[("sb", s, jj)][:, half * 256:(half + 1) * 256], lhsT=xT[:, 256 + j * P:256 + (j + 1) * P], rhs=xT[:, 0:256], start=True, stop=True)
+
+        def pre_a(s):
             na = wk.tile([P, 2], F32, name="na", bufs=4)
-            nb = wk.tile([P, 2], F32, name="nb", bufs=4)
-            xs = []
+            st[("na", s)] = na
             for jj in range(2):
                 x = wk.tile([P, 512], F32, name="x", bufs=6)
-                xs.append(x)
                 st[("x", s, jj)] = x
                 nc.vector.tensor_scalar(out=x[:].rearrange("p (u k e) -> p u k e", u=2, e=2)[:, :, 0:64, :],
                                         in0=st[("sb", s, jj)][:, 0:256].rearrange("p (e k u) -> p u k e", e=2, u=2),
                                         scalar1=-C, scalar2=None, op0=ALU.mult, op1=ALU.min, accum_out=na[:, jj:jj + 1])
+
+        def pre_t(s):
+            na = st[("na", s)]
+            nb = wk.tile([P, 2], F32, name="nb", bufs=4)
             for jj in range(2):
-                nc.vector.tensor_scalar(out=xs[jj][:].rearrange("p (u k e) -> p u k e", u=2, e=2)[:, :, 64:128, :],
+                nc.vector.tensor_scalar(out=st[("x", s, jj)][:].rearrange("p (u k e) -> p u k e", u=2, e=2)[:, :, 64:128, :],
                                         in0=st[("sb", s, jj)][:, 256:512].rearrange("p (e k u) -> p u k e", e=2, u=2),
                                         scalar1=ncr[:, 0:1], scalar2=na[:, jj:jj + 1], op0=ALU.mult, op1=ALU.min, accum_out=nb[:, jj:jj + 1])
             st[("nb", s)] = nb
@@ -161,32 +179,40 @@ def tile_l1regressionmoeactionhead_pb_kernel(tc, q_a, q_t, k_a, k_t, v_a, v_t, g
                                      bias=nb[:, jj:jj + 1], scale=-1.0, accum_out=st[("rs", h)][:, j:j + 1])
             st[("e", s)] = e
 
-        def te(s):
+        def te(s, j0=0, j1=2, warm=False):
             words = st[("e", s)][:].bitcast(F32)
             t2 = ps_t.tile([P, 512], F32, name="tt")
-            for i in range(4):
+            if warm:
+                keep_warm(t2)
+            for i in range(2 * j0, 2 * j1):
                 nc.tensor.transpose(t2[:, i * P:(i + 1) * P], words[:, i * P:(i + 1) * P], ident32[:])
-            st[("t2", s)] = t2
+            st[("t2", s, j0)] = t2
 
-        def ev(s):
-            if s % 2 == 0:
+        def ev(s, j0=0, j1=2, vec=False):
+            if s % 2 == 0 and j0 == 0:
                 gr = wk.tile([P, 2048], BF16, name="gr", align_bytes=64, bufs=3)
                 st[("gr", s // 2)] = gr
             b0 = (s % 2) * 512
-            nc.scalar.copy(out=st[("gr", s // 2)][:].bitcast(F32)[:, b0:b0 + 512].rearrange("p (j q u) -> p j q u", j=2, u=2),
-                           in_=st[("t2", s)][:].rearrange("p (j u q) -> p j q u", j=2, u=2))
+            dst = st[("gr", s // 2)][:].bitcast(F32)[:, b0 + j0 * 256:b0 + j1 * 256].rearrange("p (j q u) -> p j q u", q=P, u=2)
+            src = st[("t2", s, j0)][:, j0 * 256:j1 * 256].rearrange("p (j u q) -> p j q u", u=2, q=P)
+            if vec:
+                nc.vector.tensor_copy(out=dst, in_=src)
+            else:
+                nc.scalar.copy(out=dst, in_=src)
 
-        def qz(h):
-            codes = wk.tile([P, 512], U32, name="codes", align_bytes=64, bufs=3)
-            scl = wk.tile([P, 512], U8, name="scl", align_bytes=64, bufs=3)
-            nc.vector.quantize_mx(out=codes[:].bitcast(FP8X4), scales=scl[:], in_=st[("gr", h)][:])
-            st[("cd", h)] = (codes, scl)
-
-        def mx(h):
-            o = ps_t.tile([P, 512], F32, name="tt")
-            st[("o", h)] = o
+        def qz(h, j0=0, j1=4):
+            if j0 == 0:
+                codes = wk.tile([P, 512], U32, name="codes", align_bytes=64, bufs=3)
+                scl = wk.tile([P, 512], U8, name="scl", align_bytes=64, bufs=3)
+                st[("cd", h)] = (codes, scl)
             codes, scl = st[("cd", h)]
-            for j in range(4):
+            nc.vector.quantize_mx(out=codes[:, j0 * P:j1 * P].bitcast(FP8X4), scales=scl[:, j0 * P:j1 * P], in_=st[("gr", h)][:, j0 * 512:j1 * 512])
+
+        def mx(h, j0=0, j1=4):
+            o = ps_t.tile([P, 512], F32, name="tt")
+            st[("o", h, j0)] = o
+            codes, scl = st[("cd", h)]
+            for j in range(j0, j1):
                 nc.tensor.matmul_mx(
                     out=o[:, j * D:(j + 1) * D],
                     lhsT=codes[:, j * P:(j + 1) * P].bitcast(FP8X4),
@@ -196,47 +222,115 @@ def tile_l1regressionmoeactionhead_pb_kernel(tc, q_a, q_t, k_a, k_t, v_a, v_t, g
                     start=True, stop=True,
                 )
 
-        def recip(h):
-            rinv = wk.tile([P, 4], F32, name="rinv", bufs=4)
-            nc.vector.reciprocal(out=rinv[:], in_=st[("rs", h)][:])
-            st[("rinv", h)] = rinv
+        def recip(h, j0=0, j1=4):
+            if j0 == 0:
+                rinv = wk.tile([P, 4], F32, name="rinv", bufs=4)
+                st[("rinv", h)] = rinv
+            nc.vector.reciprocal(out=st[("rinv", h)][:, j0:j1], in_=st[("rs", h)][:, j0:j1])
 
-        def nm(h):
+        def nm(h, j0=0, j1=4, vec=True):
             osb = wk.tile([P, 512], F32, name="osb", bufs=4)
-            nc.vector.tensor_tensor(out=osb[:].rearrange("p (j d) -> p j d", d=D), in0=st[("o", h)][:].rearrange("p (j d) -> p j d", d=D),
-                                    in1=st[("rinv", h)][:].unsqueeze(2).to_broadcast([P, 4, D]), op=ALU.mult)
+            o = st[("o", h, j0)]
+            rinv = st[("rinv", h)]
+            if vec:
+                nc.vector.tensor_tensor(out=osb[:, j0 * D:j1 * D].rearrange("p (j d) -> p j d", d=D), in0=o[:, j0 * D:j1 * D].rearrange("p (j d) -> p j d", d=D),
+                                        in1=rinv[:, j0:j1].unsqueeze(2).to_broadcast([P, j1 - j0, D]), op=ALU.mult)
+            else:
+                for j in range(j0, j1):
+                    nc.scalar.activation(out=osb[:, j * D:(j + 1) * D], in_=o[:, j * D:(j + 1) * D], func=ACT.Copy, scale=rinv[:, j:j + 1])
             n, hh = divmod(h, 8)
             nc.sync.dma_start(
-                out=out[n].rearrange("(p j) c -> p j c", j=4)[:, :, hh * D:(hh + 1) * D],
-                in_=osb[:].rearrange("p (j d) -> p j d", d=D),
+                out=out[n].rearrange("(p j) c -> p j c", j=4)[:, j0:j1, hh * D:(hh + 1) * D],
+                in_=osb[:, j0 * D:j1 * D].rearrange("p (j d) -> p j d", d=D),
             )
 
-        for t in range(-6, NPAIR + 5):
-            if 0 <= t - 1 < NPAIR:
-                te(t - 1)
-            if t % 2 == 0 and 0 <= (t - 4) // 2 < HEADS:
-                mx((t - 4) // 2)
-            if 0 <= t + 2 < NPAIR:
+        for jj in range(2):
+            bank(0, jj)
+        for i in range(NWARM):
+            nc.tensor.matmul(out=st[("sb", 0, i % 2)][:], lhsT=zeros[:, 0:P], rhs=zeros[:], start=True, stop=True)
+        t1_pe(0, 0, 4)
+        t1_pe(1, 0, 4)
+        t1_ev(0, 0, 4, vec=True)
+        t1_ev(1, 0, 4)
+        sc(0, 0, (0,))
+        sc(0, 1, (0,))
+        t1_pe(0, 4, 6)
+        t1_pe(1, 4, 6)
+        pre_a(0)
+        gate()
+        sc(0, 0, (1,))
+        sc(0, 1, (1,))
+        t1_ev(0, 4, 6)
+        t1_ev(1, 4, 6)
+        t1_pe(2)
+        pre_t(0)
+        t1_ev(2)
+        vprep(0)
+        vprep(1)
+        bank(1, 0)
+        bank(1, 1)
+        sc(1, 0)
+        sc(1, 1)
+        t1_pe(3)
+        t1_pe(4)
+
+        last = HEADS - 1
+        for t in range(NPAIR + 1):
+            if 0 < t and t + 2 < NPAIR:
+                bank(t + 2, 0)
+                bank(t + 2, 1)
                 sc(t + 2, 0)
                 sc(t + 2, 1)
-            if 0 <= t + 6 < NSET:
-                t1_pe(t + 6)
-            if 0 <= t + 1 < NPAIR:
-                pre(t + 1)
-            if t % 2 == 1 and 0 <= (t - 3) // 2 < HEADS:
+            if t % 2 == 0 and 4 <= t < NPAIR:
+                mx((t - 4) // 2)
+            if 1 <= t < NPAIR:
+                te(t - 1, warm=t % 2 == 1 and 2 < t)
+            if t == NPAIR:
+                te(t - 1, 0, 1)
+                te(t - 1, 1, 2)
+                mx((t - 4) // 2)
+            if t + 5 < NSET:
+                t1_pe(t + 5)
+            if t + 1 < NPAIR:
+                pre_a(t + 1)
+                pre_t(t + 1)
+            if t % 2 == 1 and t >= 3:
                 qz((t - 3) // 2)
                 recip((t - 3) // 2)
-            if (t - 2) % 8 == 0 and 0 <= (t - 2) // 8 < HEADS // 4:
+            if (t - 2) % 8 == 0:
                 vquant((t - 2) // 8)
-            if t % 2 == 0 and 0 <= (t - 4) // 2 < HEADS:
+            if t % 2 == 0 and t >= 4 and (t - 4) // 2 not in NM_S:
                 nm((t - 4) // 2)
-            if t < 0 and 0 <= t + 5 < NSET:
-                t1_ev(t + 5)
-            if 0 <= t < NPAIR:
+            if t >= 1 and t + 4 < NSET:
+                t1_ev(t + 4)
+            if t < NPAIR:
                 ex(t)
-            if 0 <= t - 1 < NPAIR:
-                ev(t - 1)
-            if t >= 0 and 0 <= t + 5 < NSET:
-                t1_ev(t + 5)
-            if 0 <= t + 3 < HEADS:
-                vprep(t + 3)
+            if t == NPAIR:
+                break
+            if t >= 1:
+                ev(t - 1, vec=t >= NPAIR - 2)
+            if t == 0:
+                t1_ev(3)
+                bank(2, 0)
+                bank(2, 1)
+                sc(2, 0)
+                sc(2, 1)
+                t1_ev(4)
+            if t % 2 == 0 and t >= 4 and (t - 4) // 2 in NM_S:
+                nm((t - 4) // 2, vec=False)
+            if t + 2 < HEADS:
+                vprep(t + 2)
+
+        qz(last, 0, 2)
+        recip(last, 0, 2)
+        ev(NPAIR - 1, 0, 1, vec=True)
+        ev(NPAIR - 1, 1, 2)
+        mx(last, 0, 2)
+        qz(last, 2, 3)
+        recip(last, 2, 4)
+        mx(last, 2, 3)
+        nm(last, 0, 2)
+        qz(last, 3, 4)
+        mx(last, 3, 4)
+        nm(last, 2, 3)
+        nm(last, 3, 4, vec=False)

@@ -22,7 +22,7 @@ NSET = 2 * HEADS
 C = 1.0 / math.sqrt(128.0)
 FLOPS = 4 * HEADS * T * (2 * KS) * D
 NWARM = 3
-NM_S = (1, 4, 7, 10)
+NM_S = ()
 CHUNKS = ((2, 4), (4, 8), (8, 12), (12, 16))
 
 

@@ -11,6 +11,7 @@ U8 = mybir.dt.uint8
 FP8X4 = mybir.dt.float8_e4m3fn_x4
 ALU = mybir.AluOpType
 ACT = mybir.ActivationFunctionType
+AX = mybir.AxisListType
 
 P = 128
 HEADS = 16
@@ -23,6 +24,7 @@ C = 1.0 / math.sqrt(128.0)
 FLOPS = 4 * HEADS * T * (2 * KS) * D
 NWARM = 3
 NM_S = ()
+EVV = (29,)
 CHUNKS = ((2, 4), (4, 8), (8, 12), (12, 16))
 
 
@@ -136,10 +138,6 @@ def tile_l1regressionmoeactionhead_pb_kernel(tc, q_a, q_t, k_a, k_t, v_a, v_t, g
             sb = ps_s.tile([P, 512], F32, name="sb")
             st[("sb", s, jj)] = sb
 
-        def keep_warm(t2):
-            nc.tensor.matmul_mx(out=t2[:], lhsT=vcodes[:, 0:P].bitcast(FP8X4), lhsT_scale=vscl[:, 0:P],
-                                rhs=vcodes[:, 0:512].bitcast(FP8X4), rhs_scale=vscl[:, 0:512], start=True, stop=True)
-
         def sc(s, jj, halves=(0, 1)):
             h = s // 2
             j = 2 * (s % 2) + jj
@@ -147,23 +145,22 @@ def tile_l1regressionmoeactionhead_pb_kernel(tc, q_a, q_t, k_a, k_t, v_a, v_t, g
                 xT = st[("xT", 2 * h + half)]
                 nc.tensor.matmul(out=st[("sb", s, jj)][:, half * 256:(half + 1) * 256], lhsT=xT[:, 256 + j * P:256 + (j + 1) * P], rhs=xT[:, 0:256], start=True, stop=True)
 
-        def pre_a(s):
-            na = wk.tile([P, 2], F32, name="na", bufs=4)
-            st[("na", s)] = na
+        def pre(s, half):
+            if half == 0:
+                mn = wk.tile([P, 4], F32, name="mn", bufs=4)
+                st[("mn", s)] = mn
             for jj in range(2):
-                x = wk.tile([P, 512], F32, name="x", bufs=6)
-                st[("x", s, jj)] = x
-                nc.vector.tensor_scalar(out=x[:].rearrange("p (u k e) -> p u k e", u=2, e=2)[:, :, 0:64, :],
-                                        in0=st[("sb", s, jj)][:, 0:256].rearrange("p (e k u) -> p u k e", e=2, u=2),
-                                        scalar1=-C, scalar2=None, op0=ALU.mult, op1=ALU.min, accum_out=na[:, jj:jj + 1])
+                if half == 0:
+                    x = wk.tile([P, 512], F32, name="x", bufs=6)
+                    st[("x", s, jj)] = x
+                nc.vector.tensor_scalar(out=st[("x", s, jj)][:].rearrange("p (u k e) -> p u k e", u=2, e=2)[:, :, half * 64:(half + 1) * 64, :],
+                                        in0=st[("sb", s, jj)][:, half * 256:(half + 1) * 256].rearrange("p (e k u) -> p u k e", e=2, u=2),
+                                        scalar1=-C if half == 0 else ncr[:, 0:1], scalar2=None, op0=ALU.mult, op1=ALU.min,
+                                        accum_out=st[("mn", s)][:, 2 * jj + half:2 * jj + half + 1])
 
-        def pre_t(s):
-            na = st[("na", s)]
+        def join(s):
             nb = wk.tile([P, 2], F32, name="nb", bufs=4)
-            for jj in range(2):
-                nc.vector.tensor_scalar(out=st[("x", s, jj)][:].rearrange("p (u k e) -> p u k e", u=2, e=2)[:, :, 64:128, :],
-                                        in0=st[("sb", s, jj)][:, 256:512].rearrange("p (e k u) -> p u k e", e=2, u=2),
-                                        scalar1=ncr[:, 0:1], scalar2=na[:, jj:jj + 1], op0=ALU.mult, op1=ALU.min, accum_out=nb[:, jj:jj + 1])
+            nc.vector.tensor_reduce(out=nb[:], in_=st[("mn", s)][:].rearrange("p (j h) -> p j h", h=2), axis=AX.X, op=ALU.min)
             st[("nb", s)] = nb
 
         def ex(s):
@@ -179,11 +176,9 @@ def tile_l1regressionmoeactionhead_pb_kernel(tc, q_a, q_t, k_a, k_t, v_a, v_t, g
                                      bias=nb[:, jj:jj + 1], scale=-1.0, accum_out=st[("rs", h)][:, j:j + 1])
             st[("e", s)] = e
 
-        def te(s, j0=0, j1=2, warm=False):
+        def te(s, j0=0, j1=2):
             words = st[("e", s)][:].bitcast(F32)
             t2 = ps_t.tile([P, 512], F32, name="tt")
-            if warm:
-                keep_warm(t2)
             for i in range(2 * j0, 2 * j1):
                 nc.tensor.transpose(t2[:, i * P:(i + 1) * P], words[:, i * P:(i + 1) * P], ident32[:])
             st[("t2", s, j0)] = t2
@@ -229,7 +224,7 @@ def tile_l1regressionmoeactionhead_pb_kernel(tc, q_a, q_t, k_a, k_t, v_a, v_t, g
             nc.vector.reciprocal(out=st[("rinv", h)][:, j0:j1], in_=st[("rs", h)][:, j0:j1])
 
         def nm(h, j0=0, j1=4, vec=True):
-            osb = wk.tile([P, 512], F32, name="osb", bufs=4)
+            osb = wk.tile([P, 512], F32, name="osb", bufs=6)
             o = st[("o", h, j0)]
             rinv = st[("rinv", h)]
             if vec:
@@ -256,14 +251,15 @@ def tile_l1regressionmoeactionhead_pb_kernel(tc, q_a, q_t, k_a, k_t, v_a, v_t, g
         sc(0, 1, (0,))
         t1_pe(0, 4, 6)
         t1_pe(1, 4, 6)
-        pre_a(0)
+        pre(0, 0)
         gate()
         sc(0, 0, (1,))
         sc(0, 1, (1,))
         t1_ev(0, 4, 6)
         t1_ev(1, 4, 6)
         t1_pe(2)
-        pre_t(0)
+        pre(0, 1)
+        join(0)
         t1_ev(2)
         vprep(0)
         vprep(1)
@@ -275,7 +271,7 @@ def tile_l1regressionmoeactionhead_pb_kernel(tc, q_a, q_t, k_a, k_t, v_a, v_t, g
         t1_pe(4)
 
         last = HEADS - 1
-        for t in range(NPAIR + 1):
+        for t in range(NPAIR):
             if 0 < t and t + 2 < NPAIR:
                 bank(t + 2, 0)
                 bank(t + 2, 1)
@@ -283,17 +279,13 @@ def tile_l1regressionmoeactionhead_pb_kernel(tc, q_a, q_t, k_a, k_t, v_a, v_t, g
                 sc(t + 2, 1)
             if t % 2 == 0 and 4 <= t < NPAIR:
                 mx((t - 4) // 2)
-            if 1 <= t < NPAIR:
-                te(t - 1, warm=t % 2 == 1 and 2 < t)
-            if t == NPAIR:
-                te(t - 1, 0, 1)
-                te(t - 1, 1, 2)
-                mx((t - 4) // 2)
+            if t >= 1:
+                te(t - 1)
             if t + 5 < NSET:
                 t1_pe(t + 5)
             if t + 1 < NPAIR:
-                pre_a(t + 1)
-                pre_t(t + 1)
+                pre(t + 1, 0)
+                pre(t + 1, 1)
             if t % 2 == 1 and t >= 3:
                 qz((t - 3) // 2)
                 recip((t - 3) // 2)
@@ -301,14 +293,13 @@ def tile_l1regressionmoeactionhead_pb_kernel(tc, q_a, q_t, k_a, k_t, v_a, v_t, g
                 vquant((t - 2) // 8)
             if t % 2 == 0 and t >= 4 and (t - 4) // 2 not in NM_S:
                 nm((t - 4) // 2)
+            if t + 1 < NPAIR:
+                join(t + 1)
             if t >= 1 and t + 4 < NSET:
                 t1_ev(t + 4)
-            if t < NPAIR:
-                ex(t)
-            if t == NPAIR:
-                break
+            ex(t)
             if t >= 1:
-                ev(t - 1, vec=t >= NPAIR - 2)
+                ev(t - 1, vec=(t - 1) in EVV)
             if t == 0:
                 t1_ev(3)
                 bank(2, 0)
@@ -321,16 +312,19 @@ def tile_l1regressionmoeactionhead_pb_kernel(tc, q_a, q_t, k_a, k_t, v_a, v_t, g
             if t + 2 < HEADS:
                 vprep(t + 2)
 
-        qz(last, 0, 2)
-        recip(last, 0, 2)
+        te(NPAIR - 1, 0, 1)
+        te(NPAIR - 1, 1, 2)
+        mx(last - 1)
         ev(NPAIR - 1, 0, 1, vec=True)
         ev(NPAIR - 1, 1, 2)
+        qz(last, 0, 2)
+        recip(last)
         mx(last, 0, 2)
         qz(last, 2, 3)
-        recip(last, 2, 4)
         mx(last, 2, 3)
-        nm(last, 0, 2)
         qz(last, 3, 4)
         mx(last, 3, 4)
+        nm(last - 1, vec=False)
+        nm(last, 0, 2)
         nm(last, 2, 3)
         nm(last, 3, 4, vec=False)

@@ -11,7 +11,6 @@ U8 = mybir.dt.uint8
 FP8X4 = mybir.dt.float8_e4m3fn_x4
 ALU = mybir.AluOpType
 ACT = mybir.ActivationFunctionType
-AX = mybir.AxisListType
 
 P = 128
 HEADS = 16
@@ -145,22 +144,23 @@ def tile_l1regressionmoeactionhead_pb_kernel(tc, q_a, q_t, k_a, k_t, v_a, v_t, g
                 xT = st[("xT", 2 * h + half)]
                 nc.tensor.matmul(out=st[("sb", s, jj)][:, half * 256:(half + 1) * 256], lhsT=xT[:, 256 + j * P:256 + (j + 1) * P], rhs=xT[:, 0:256], start=True, stop=True)
 
-        def pre(s, half):
-            if half == 0:
-                mn = wk.tile([P, 4], F32, name="mn", bufs=4)
-                st[("mn", s)] = mn
+        def pre_a(s):
+            na = wk.tile([P, 2], F32, name="na", bufs=4)
+            st[("na", s)] = na
             for jj in range(2):
-                if half == 0:
-                    x = wk.tile([P, 512], F32, name="x", bufs=6)
-                    st[("x", s, jj)] = x
-                nc.vector.tensor_scalar(out=st[("x", s, jj)][:].rearrange("p (u k e) -> p u k e", u=2, e=2)[:, :, half * 64:(half + 1) * 64, :],
-                                        in0=st[("sb", s, jj)][:, half * 256:(half + 1) * 256].rearrange("p (e k u) -> p u k e", e=2, u=2),
-                                        scalar1=-C if half == 0 else ncr[:, 0:1], scalar2=None, op0=ALU.mult, op1=ALU.min,
-                                        accum_out=st[("mn", s)][:, 2 * jj + half:2 * jj + half + 1])
+                x = wk.tile([P, 512], F32, name="x", bufs=6)
+                st[("x", s, jj)] = x
+                nc.vector.tensor_scalar(out=x[:].rearrange("p (u k e) -> p u k e", u=2, e=2)[:, :, 0:64, :],
+                                        in0=st[("sb", s, jj)][:, 0:256].rearrange("p (e k u) -> p u k e", e=2, u=2),
+                                        scalar1=-C, scalar2=None, op0=ALU.mult, op1=ALU.min, accum_out=na[:, jj:jj + 1])
 
-        def join(s):
+        def pre_t(s):
+            na = st[("na", s)]
             nb = wk.tile([P, 2], F32, name="nb", bufs=4)
-            nc.vector.tensor_reduce(out=nb[:], in_=st[("mn", s)][:].rearrange("p (j h) -> p j h", h=2), axis=AX.X, op=ALU.min)
+            for jj in range(2):
+                nc.vector.tensor_scalar(out=st[("x", s, jj)][:].rearrange("p (u k e) -> p u k e", u=2, e=2)[:, :, 64:128, :],
+                                        in0=st[("sb", s, jj)][:, 256:512].rearrange("p (e k u) -> p u k e", e=2, u=2),
+                                        scalar1=ncr[:, 0:1], scalar2=na[:, jj:jj + 1], op0=ALU.mult, op1=ALU.min, accum_out=nb[:, jj:jj + 1])
             st[("nb", s)] = nb
 
         def ex(s):
@@ -247,20 +247,20 @@ def tile_l1regressionmoeactionhead_pb_kernel(tc, q_a, q_t, k_a, k_t, v_a, v_t, g
         t1_pe(1, 0, 4)
         t1_ev(0, 0, 4, vec=True)
         t1_ev(1, 0, 4)
+        nc.tensor.matmul(out=st[("sb", 0, 0)][:], lhsT=zeros[:, 0:P], rhs=zeros[:], start=True, stop=True)
         sc(0, 0, (0,))
         sc(0, 1, (0,))
         t1_pe(0, 4, 6)
         t1_pe(1, 4, 6)
-        pre(0, 0)
+        pre_a(0)
         gate()
         sc(0, 0, (1,))
         sc(0, 1, (1,))
         t1_ev(0, 4, 6)
         t1_ev(1, 4, 6)
         t1_pe(2)
-        pre(0, 1)
-        join(0)
-        t1_ev(2)
+        pre_t(0)
+        t1_ev(2, vec=True)
         vprep(0)
         vprep(1)
         bank(1, 0)
@@ -284,8 +284,8 @@ def tile_l1regressionmoeactionhead_pb_kernel(tc, q_a, q_t, k_a, k_t, v_a, v_t, g
             if t + 5 < NSET:
                 t1_pe(t + 5)
             if t + 1 < NPAIR:
-                pre(t + 1, 0)
-                pre(t + 1, 1)
+                pre_a(t + 1)
+                pre_t(t + 1)
             if t % 2 == 1 and t >= 3:
                 qz((t - 3) // 2)
                 recip((t - 3) // 2)
@@ -293,8 +293,6 @@ def tile_l1regressionmoeactionhead_pb_kernel(tc, q_a, q_t, k_a, k_t, v_a, v_t, g
                 vquant((t - 2) // 8)
             if t % 2 == 0 and t >= 4 and (t - 4) // 2 not in NM_S:
                 nm((t - 4) // 2)
-            if t + 1 < NPAIR:
-                join(t + 1)
             if t >= 1 and t + 4 < NSET:
                 t1_ev(t + 4)
             ex(t)

@@ -24,7 +24,6 @@ FLOPS = 4 * HEADS * T * (2 * KS) * D
 NWARM = 3
 NM_S = ()
 EVV = (29,)
-CHUNKS = ((2, 4), (4, 8), (8, 12), (12, 16))
 
 
 def tile_l1regressionmoeactionhead_pb_kernel(tc, q_a, q_t, k_a, k_t, v_a, v_t, gating_factor, out):
@@ -78,11 +77,13 @@ def tile_l1regressionmoeactionhead_pb_kernel(tc, q_a, q_t, k_a, k_t, v_a, v_t, g
 
         nc.scalar.dma_start(out=g_sb[:], in_=gating_factor.partition_broadcast(P))
         load_kq(0, 1)
-        load_kq(1, 2)
-        load_v(0, 2)
-        for h0, h1 in CHUNKS:
-            load_kq(h0, h1)
-            load_v(h0, h1)
+        load_kq(1, 3)
+        load_v(0, 4)
+        load_kq(3, 6)
+        load_v(4, 8)
+        load_kq(6, 10)
+        load_v(8, 16)
+        load_kq(10, 16)
 
         make_identity(nc, ident[:])
         make_identity(nc, ident32[:])
@@ -225,7 +226,7 @@ def tile_l1regressionmoeactionhead_pb_kernel(tc, q_a, q_t, k_a, k_t, v_a, v_t, g
 
         def nm(h, j0=0, j1=4, vec=True):
             osb = wk.tile([P, 512], F32, name="osb", bufs=6)
-            o = st[("o", h, j0)]
+            o = st[("o", h, j0 if h == HEADS - 1 else 0)]
             rinv = st[("rinv", h)]
             if vec:
                 nc.vector.tensor_tensor(out=osb[:, j0 * D:j1 * D].rearrange("p (j d) -> p j d", d=D), in0=o[:, j0 * D:j1 * D].rearrange("p (j d) -> p j d", d=D),
@@ -289,8 +290,8 @@ def tile_l1regressionmoeactionhead_pb_kernel(tc, q_a, q_t, k_a, k_t, v_a, v_t, g
             if t % 2 == 1 and t >= 3:
                 qz((t - 3) // 2)
                 recip((t - 3) // 2)
-            if (t - 2) % 8 == 0:
-                vquant((t - 2) // 8)
+            if (t - 3) % 8 == 0:
+                vquant((t - 3) // 8)
             if t % 2 == 0 and t >= 4 and (t - 4) // 2 not in NM_S:
                 nm((t - 4) // 2)
             if t >= 1 and t + 4 < NSET:
@@ -322,7 +323,8 @@ def tile_l1regressionmoeactionhead_pb_kernel(tc, q_a, q_t, k_a, k_t, v_a, v_t, g
         mx(last, 2, 3)
         qz(last, 3, 4)
         mx(last, 3, 4)
-        nm(last - 1, vec=False)
+        nm(last - 1, 0, 2, vec=False)
+        nm(last - 1, 2, 4)
         nm(last, 0, 2)
         nm(last, 2, 3)
         nm(last, 3, 4, vec=False)

@@ -104,7 +104,7 @@ def tile_l1regressionmoeactionhead_pb_kernel(tc, q_a, q_t, k_a, k_t, v_a, v_t, g
 
         def t1_ev(n, lo=0, hi=6, vec=False):
             if lo == 0:
-                xT = wk.tile([P, 768], BF16, name="xT%d" % (n % 2), bufs=3)
+                xT = wk.tile([P, 768], BF16, name="xT%d" % (n % 2), bufs=4)
                 st[("xT", n)] = xT
             dst = st[("xT", n)][:, lo * P:hi * P]
             src = st[("t1", n, lo)][:, lo * P:hi * P]
@@ -273,17 +273,19 @@ def tile_l1regressionmoeactionhead_pb_kernel(tc, q_a, q_t, k_a, k_t, v_a, v_t, g
 
         last = HEADS - 1
         for t in range(NPAIR):
+            if t >= 1:
+                te(t - 1)
+            if t % 2 == 0 and 4 <= t < NPAIR:
+                mx((t - 4) // 2)
             if 0 < t and t + 2 < NPAIR:
                 bank(t + 2, 0)
                 bank(t + 2, 1)
                 sc(t + 2, 0)
                 sc(t + 2, 1)
-            if t % 2 == 0 and 4 <= t < NPAIR:
-                mx((t - 4) // 2)
-            if t >= 1:
-                te(t - 1)
             if t + 5 < NSET:
                 t1_pe(t + 5)
+            if t % 2 == 1 and t >= 5:
+                nm((t - 5) // 2)
             if t + 1 < NPAIR:
                 pre_a(t + 1)
                 pre_t(t + 1)
@@ -292,11 +294,9 @@ def tile_l1regressionmoeactionhead_pb_kernel(tc, q_a, q_t, k_a, k_t, v_a, v_t, g
                 recip((t - 3) // 2)
             if (t - 3) % 8 == 0:
                 vquant((t - 3) // 8)
-            if t % 2 == 0 and t >= 4 and (t - 4) // 2 not in NM_S:
-                nm((t - 4) // 2)
+            ex(t)
             if t >= 1 and t + 4 < NSET:
                 t1_ev(t + 4)
-            ex(t)
             if t >= 1:
                 ev(t - 1, vec=(t - 1) in EVV)
             if t == 0:

import math
from contextlib import ExitStack

import concourse.mybir as mybir
from concourse.masks import make_identity

BF16 = mybir.dt.bfloat16
F32 = mybir.dt.float32
U32 = mybir.dt.uint32
U8 = mybir.dt.uint8
FP8X4 = mybir.dt.float8_e4m3fn_x4
ALU = mybir.AluOpType
ACT = mybir.ActivationFunctionType

P = 128
HEADS = 16
T = 512
KS = 256
D = 128
NPAIR = 2 * HEADS
NSET = 2 * HEADS
C = 1.0 / math.sqrt(128.0)
FLOPS = 4 * HEADS * T * (2 * KS) * D
NWARM = 3
NM_S = ()
EVV = (29,)


def tile_l1regressionmoeactionhead_pb_kernel(tc, q_a, q_t, k_a, k_t, v_a, v_t, gating_factor, out):
    nc = tc.nc
    with ExitStack() as ctx:
        ctx.enter_context(tc.manual_schedule())
        res = ctx.enter_context(tc.tile_pool(name="res", bufs=1))
        wk = ctx.enter_context(tc.tile_pool(name="wk", bufs=3))
        ps_s = ctx.enter_context(tc.psum_pool(name="ps_s", bufs=4))
        ps_t = ctx.enter_context(tc.psum_pool(name="ps_t", bufs=4))

        g_sb = res.tile([P, 1], BF16)
        qa_sb = res.tile([P, HEADS * 512], BF16)
        qt_sb = res.tile([P, HEADS * 512], BF16)
        ka_sb = res.tile([P, HEADS * 256], BF16)
        kt_sb = res.tile([P, HEADS * 256], BF16)
        v_sb = res.tile([P, HEADS * 512], BF16)
        vcodes = res.tile([P, HEADS * D], U32, align_bytes=64)
        vscl = res.tile([P, HEADS * D], U8, align_bytes=64)
        ident = res.tile([P, P], BF16)
        zeros = res.tile([P, 512], BF16)
        ident32 = res.tile([P, P], F32)
        eg = res.tile([P, 1], F32)
        dummy = res.tile([P, 1], F32)
        eg1 = res.tile([P, 1], F32)
        ratio = res.tile([P, 1], F32)
        ncr = res.tile([P, 1], F32)

        qa_v = q_a.rearrange("b h (p j) d -> p (b h) (j d)", j=4)
        qt_v = q_t.rearrange("b h (p j) d -> p (b h) (j d)", j=4)
        ka_v = k_a.rearrange("b h (p j) d -> p (b h) (j d)", j=2)
        kt_v = k_t.rearrange("b h (p j) d -> p (b h) (j d)", j=2)
        va_v = v_a.rearrange("b h (p t) d -> p (b h) (t d)", t=4)
        vt_v = v_t.rearrange("b h (p t) d -> p (b h) (t d)", t=4)
        qa_s = qa_sb[:].rearrange("p (h x) -> p h x", x=512)
        qt_s = qt_sb[:].rearrange("p (h x) -> p h x", x=512)
        ka_s = ka_sb[:].rearrange("p (h x) -> p h x", x=256)
        kt_s = kt_sb[:].rearrange("p (h x) -> p h x", x=256)
        v_s = v_sb[:].rearrange("p (h x) -> p h x", x=512)
        v_r = v_sb[:].rearrange("p (h t d) -> p h d t", t=4, d=D)

        def load_kq(h0, h1):
            nc.sync.dma_start(out=ka_s[:, h0:h1, :], in_=ka_v[:, h0:h1, :])
            nc.sync.dma_start(out=qa_s[:, h0:h1, :], in_=qa_v[:, h0:h1, :])
            nc.sync.dma_start(out=kt_s[:, h0:h1, :], in_=kt_v[:, h0:h1, :])
            nc.sync.dma_start(out=qt_s[:, h0:h1, :], in_=qt_v[:, h0:h1, :])

        def load_v(h0, h1):
            nc.sync.dma_start(out=v_s[0:64, h0:h1, :], in_=va_v[:, h0:h1, :])
            nc.sync.dma_start(out=v_s[64:128, h0:h1, :], in_=vt_v[:, h0:h1, :])

        nc.scalar.dma_start(out=g_sb[:], in_=gating_factor.partition_broadcast(P))
        load_kq(0, 1)
        load_kq(1, 3)
        load_v(0, 4)
        load_kq(3, 6)
        load_v(4, 8)
        load_kq(6, 10)
        load_v(8, 16)
        load_kq(10, 16)

        make_identity(nc, ident[:])
        make_identity(nc, ident32[:])
        nc.vector.memset(zeros[:], 0.0)
        nc.vector.memset(eg[:], 0.0)
        nc.scalar.activation(out=dummy[:], in_=eg[:], func=ACT.Exp)

        st = {}

        def t1_pe(n, lo=0, hi=6):
            h, s = divmod(n, 2)
            q_sb, k_sb = (qa_sb, ka_sb) if s == 0 else (qt_sb, kt_sb)
            t1 = ps_t.tile([P, 1024], BF16, name="tt")
            for i in range(lo, hi):
                src = k_sb[:, h * 256 + i * P:h * 256 + (i + 1) * P] if i < 2 else q_sb[:, h * 512 + (i - 2) * P:h * 512 + (i - 1) * P]
                nc.tensor.transpose(t1[:, i * P:(i + 1) * P], src, ident[:])
            st[("t1", n, lo)] = t1

        def t1_ev(n, lo=0, hi=6, vec=False):
            if lo == 0:
                xT = wk.tile([P, 768], BF16, name="xT%d" % (n % 2), bufs=4)
                st[("xT", n)] = xT
            dst = st[("xT", n)][:, lo * P:hi * P]
            src = st[("t1", n, lo)][:, lo * P:hi * P]
            if vec:
                nc.vector.tensor_copy(out=dst, in_=src)
            else:
                nc.scalar.copy(out=dst, in_=src)

        def gate():
            nc.scalar.activation(out=eg[:], in_=g_sb[:], func=ACT.Exp, scale=-1.0)
            nc.vector.tensor_scalar_add(out=eg1[:], in0=eg[:], scalar1=1.0)
            nc.vector.reciprocal(out=ratio[:], in_=eg1[:])
            nc.vector.tensor_scalar_mul(out=ncr[:], in0=ratio[:], scalar1=-C)

        def vprep(h):
            if h % 4 == 0:
                vg = wk.tile([P, 2048], BF16, name="vg", align_bytes=64, bufs=4)
                st[("vg", h // 4)] = vg
            lo = (h % 4) * 512
            nc.gpsimd.tensor_scalar(out=st[("vg", h // 4)][:, lo:lo + 512].rearrange("p (d t) -> p d t", t=4), in0=v_r[:, h],
                                    scalar1=1.0, scalar2=0.0, op0=ALU.mult, op1=ALU.add)

        def vquant(g):
            nc.vector.quantize_mx(
                out=vcodes[:, g * 512:(g + 1) * 512].bitcast(FP8X4),
                scales=vscl[:, g * 512:(g + 1) * 512],
                in_=st[("vg", g)][:],
            )

        def bank(s, jj):
            sb = ps_s.tile([P, 512], F32, name="sb")
            st[("sb", s, jj)] = sb

        def sc(s, jj, halves=(0, 1)):
            h = s // 2
            j = 2 * (s % 2) + jj
            for half in halves:
                xT = st[("xT", 2 * h + half)]
                nc.tensor.matmul(out=st[("sb", s, jj)][:, half * 256:(half + 1) * 256], lhsT=xT[:, 256 + j * P:256 + (j + 1) * P], rhs=xT[:, 0:256], start=True, stop=True)

        def pre_a(s):
            na = wk.tile([P, 2], F32, name="na", bufs=4)
            st[("na", s)] = na
            for jj in range(2):
                x = wk.tile([P, 512], F32, name="x", bufs=6)
                st[("x", s, jj)] = x
                nc.vector.tensor_scalar(out=x[:].rearrange("p (u k e) -> p u k e", u=2, e=2)[:, :, 0:64, :],
                                        in0=st[("sb", s, jj)][:, 0:256].rearrange("p (e k u) -> p u k e", e=2, u=2),
                                        scalar1=-C, scalar2=None, op0=ALU.mult, op1=ALU.min, accum_out=na[:, jj:jj + 1])

        def pre_t(s):
            na = st[("na", s)]
            nb = wk.tile([P, 2], F32, name="nb", bufs=4)
            for jj in range(2):
                nc.vector.tensor_scalar(out=st[("x", s, jj)][:].rearrange("p (u k e) -> p u k e", u=2, e=2)[:, :, 64:128, :],
                                        in0=st[("sb", s, jj)][:, 256:512].rearrange("p (e k u) -> p u k e", e=2, u=2),
                                        scalar1=ncr[:, 0:1], scalar2=na[:, jj:jj + 1], op0=ALU.mult, op1=ALU.min, accum_out=nb[:, jj:jj + 1])
            st[("nb", s)] = nb

        def ex(s):
            h = s // 2
            if s % 2 == 0:
                rs = wk.tile([P, 4], F32, name="rs", bufs=4)
                st[("rs", h)] = rs
            nb = st[("nb", s)]
            e = wk.tile([P, 1024], BF16, name="e", bufs=3)
            for jj in range(2):
                j = 2 * (s % 2) + jj
                nc.scalar.activation(out=e[:, jj * 512:(jj + 1) * 512], in_=st[("x", s, jj)][:], func=ACT.Exp,
                                     bias=nb[:, jj:jj + 1], scale=-1.0, accum_out=st[("rs", h)][:, j:j + 1])
            st[("e", s)] = e

        def te(s, j0=0, j1=2):
            words = st[("e", s)][:].bitcast(F32)
            t2 = ps_t.tile([P, 512], F32, name="tt")
            for i in range(2 * j0, 2 * j1):
                nc.tensor.transpose(t2[:, i * P:(i + 1) * P], words[:, i * P:(i + 1) * P], ident32[:])
            st[("t2", s, j0)] = t2

        def ev(s, j0=0, j1=2, vec=False):
            if s % 2 == 0 and j0 == 0:
                gr = wk.tile([P, 2048], BF16, name="gr", align_bytes=64, bufs=3)
                st[("gr", s // 2)] = gr
            b0 = (s % 2) * 512
            dst = st[("gr", s // 2)][:].bitcast(F32)[:, b0 + j0 * 256:b0 + j1 * 256].rearrange("p (j q u) -> p j q u", q=P, u=2)
            src = st[("t2", s, j0)][:, j0 * 256:j1 * 256].rearrange("p (j u q) -> p j q u", u=2, q=P)
            if vec:
                nc.vector.tensor_copy(out=dst, in_=src)
            else:
                nc.scalar.copy(out=dst, in_=src)

        def qz(h, j0=0, j1=4):
            if j0 == 0:
                codes = wk.tile([P, 512], U32, name="codes", align_bytes=64, bufs=3)
                scl = wk.tile([P, 512], U8, name="scl", align_bytes=64, bufs=3)
                st[("cd", h)] = (codes, scl)
            codes, scl = st[("cd", h)]
            nc.vector.quantize_mx(out=codes[:, j0 * P:j1 * P].bitcast(FP8X4), scales=scl[:, j0 * P:j1 * P], in_=st[("gr", h)][:, j0 * 512:j1 * 512])

        def mx(h, j0=0, j1=4):
            o = ps_t.tile([P, 512], F32, name="tt")
            st[("o", h, j0)] = o
            codes, scl = st[("cd", h)]
            for j in range(j0, j1):
                nc.tensor.matmul_mx(
                    out=o[:, j * D:(j + 1) * D],
                    lhsT=codes[:, j * P:(j + 1) * P].bitcast(FP8X4),
                    lhsT_scale=scl[:, j * P:(j + 1) * P],
                    rhs=vcodes[:, h * D:(h + 1) * D].bitcast(FP8X4),
                    rhs_scale=vscl[:, h * D:(h + 1) * D],
                    start=True, stop=True,
                )

        def recip(h, j0=0, j1=4):
            if j0 == 0:
                rinv = wk.tile([P, 4], F32, name="rinv", bufs=4)
                st[("rinv", h)] = rinv
            nc.vector.reciprocal(out=st[("rinv", h)][:, j0:j1], in_=st[("rs", h)][:, j0:j1])

        def nm(h, j0=0, j1=4, vec=True):
            osb = wk.tile([P, 512], F32, name="osb", bufs=6)
            o = st[("o", h, j0 if h == HEADS - 1 else 0)]
            rinv = st[("rinv", h)]
            if vec:
                nc.vector.tensor_tensor(out=osb[:, j0 * D:j1 * D].rearrange("p (j d) -> p j d", d=D), in0=o[:, j0 * D:j1 * D].rearrange("p (j d) -> p j d", d=D),
                                        in1=rinv[:, j0:j1].unsqueeze(2).to_broadcast([P, j1 - j0, D]), op=ALU.mult)
            else:
                for j in range(j0, j1):
                    nc.scalar.activation(out=osb[:, j * D:(j + 1) * D], in_=o[:, j * D:(j + 1) * D], func=ACT.Copy, scale=rinv[:, j:j + 1])
            n, hh = divmod(h, 8)
            nc.sync.dma_start(
                out=out[n].rearrange("(p j) c -> p j c", j=4)[:, j0:j1, hh * D:(hh + 1) * D],
                in_=osb[:, j0 * D:j1 * D].rearrange("p (j d) -> p j d", d=D),
            )

        for jj in range(2):
            bank(0, jj)
        for i in range(NWARM):
            nc.tensor.matmul(out=st[("sb", 0, i % 2)][:], lhsT=zeros[:, 0:P], rhs=zeros[:], start=True, stop=True)
        t1_pe(0, 0, 4)
        t1_pe(1, 0, 4)
        t1_ev(0, 0, 4, vec=True)
        t1_ev(1, 0, 4)
        nc.tensor.matmul(out=st[("sb", 0, 0)][:], lhsT=zeros[:, 0:P], rhs=zeros[:], start=True, stop=True)
        sc(0, 0, (0,))
        sc(0, 1, (0,))
        t1_pe(0, 4, 6)
        t1_pe(1, 4, 6)
        pre_a(0)
        gate()
        sc(0, 0, (1,))
        sc(0, 1, (1,))
        t1_ev(0, 4, 6)
        t1_ev(1, 4, 6)
        t1_pe(2)
        pre_t(0)
        t1_ev(2, vec=True)
        vprep(0)
        vprep(1)
        bank(1, 0)
        bank(1, 1)
        sc(1, 0)
        sc(1, 1)
        t1_pe(3)
        t1_pe(4)

        last = HEADS - 1
        for t in range(NPAIR):
            if t >= 1:
                te(t - 1)
            if t % 2 == 0 and 4 <= t < NPAIR:
                mx((t - 4) // 2)
            if 0 < t and t + 2 < NPAIR:
                bank(t + 2, 0)
                bank(t + 2, 1)
                sc(t + 2, 0)
                sc(t + 2, 1)
            if t + 5 < NSET:
                t1_pe(t + 5)
            if t % 2 == 1 and t >= 5:
                nm((t - 5) // 2)
            if t + 1 < NPAIR:
                pre_a(t + 1)
                pre_t(t + 1)
            if t % 2 == 1 and t >= 3:
                qz((t - 3) // 2)
                recip((t - 3) // 2)
            if (t - 3) % 8 == 0:
                vquant((t - 3) // 8)
            ex(t)
            if t >= 1 and t + 4 < NSET:
                t1_ev(t + 4)
            if t >= 1:
                ev(t - 1, vec=(t - 1) in EVV)
            if t == 0:
                t1_ev(3)
                bank(2, 0)
                bank(2, 1)
                sc(2, 0)
                sc(2, 1)
                t1_ev(4)
            if t % 2 == 0 and t >= 4 and (t - 4) // 2 in NM_S:
                nm((t - 4) // 2, vec=False)
            if t + 2 < HEADS:
                vprep(t + 2)

        te(NPAIR - 1, 0, 1)
        te(NPAIR - 1, 1, 2)
        mx(last - 1)
        ev(NPAIR - 1, 0, 1, vec=True)
        ev(NPAIR - 1, 1, 2)
        qz(last, 0, 2)
        recip(last)
        mx(last, 0, 2)
        qz(last, 2, 3)
        mx(last, 2, 3)
        qz(last, 3, 4)
        mx(last, 3, 4)
        nm(last - 1, 0, 2, vec=False)
        nm(last - 1, 2, 4)
        nm(last, 0, 2)
        nm(last, 2, 3)
        nm(last, 3, 4, vec=False)
